import numpy as np
import ml_dtypes


def mxq(x, axis, fmt="e4m3"):
    dtype, down = {"e4m3": (ml_dtypes.float8_e4m3fn, 7), "e5m2": (ml_dtypes.float8_e5m2, 14)}[fmt]
    v = np.moveaxis(np.asarray(x, np.float32).astype(ml_dtypes.bfloat16).astype(np.float64), axis, -1)
    blocks = v.reshape(v.shape[:-1] + (-1, 32))
    amax = np.abs(blocks).max(-1, keepdims=True)
    byte = np.maximum(np.where(amax > 0, np.frexp(amax)[1] - 1 + 127, 0) - down, 1)
    scale = np.exp2(byte - 127.0)
    codes = (blocks / scale).astype(np.float32).astype(dtype).astype(np.float64)
    return np.moveaxis((codes * scale).reshape(v.shape), -1, axis)


WIDE = False


def mx_kscale(k):
    if not WIDE:
        return np.ones(k)
    levels = np.array([10, -10, 5, -5, 0])
    if k % 512:
        return np.exp2(np.random.permutation(np.resize(levels, k // 32))).repeat(32)
    a = np.empty((k // 512, 16))
    for p in range(k // 512):
        a[p, :8] = np.random.permutation(np.resize(levels, 8))
        for g in range(8):
            far = levels[np.abs(levels - a[p, g]) >= 10]
            a[p, g + 8] = far[np.random.randint(len(far))]
    return np.exp2(a.ravel()).repeat(32)


BF16 = ml_dtypes.bfloat16


def bf(x):
    return np.asarray(x, np.float32).astype(BF16)


def f64(x):
    return np.asarray(x).astype(np.float64)


B, IN, H, C = 256, 1024, 1024, 1024
G = 4 * H


def sigmoid(v):
    return 1.0 / (1.0 + np.exp(-v))


def setup_inputs():
    si, sh, sc = mx_kscale(IN), mx_kscale(H), mx_kscale(C)
    return {
        "core_input": bf(np.random.standard_normal((B, IN)) * si),
        "h_state": bf(np.random.standard_normal((B, H)) * sh),
        "c_state": bf(np.random.standard_normal((B, H))),
        "concept": bf(np.random.random_sample((B, C)) * sc),
        "W_in": bf(np.random.standard_normal((G, IN)) * 1.0 / np.sqrt(IN) / si),
        "W_st": bf(np.random.standard_normal((G, H)) * 1.0 / np.sqrt(H) / sh),
        "W_ci": bf(np.random.standard_normal((G, C)) * 2.0 / np.sqrt(C) / sc),
        "W_cs": bf(np.random.standard_normal((G, C)) * 2.0 / np.sqrt(C) / sc),
    }


def reference(core_input, h_state, c_state, concept, W_in, W_st, W_ci, W_cs):
    cq = mxq(f64(concept), 1, "e4m3")
    gi = cq @ mxq(f64(W_ci), 1, "e4m3").T
    gs = cq @ mxq(f64(W_cs), 1, "e4m3").T
    xi = mxq(f64(core_input), 1, "e4m3") @ mxq(f64(W_in), 1, "e4m3").T
    hs = mxq(f64(h_state), 1, "e4m3") @ mxq(f64(W_st), 1, "e4m3").T
    hidden_vec = sigmoid(gi * xi + gs * hs)
    i_t, f_t, o_t, c_cand = np.split(hidden_vec, 4, axis=1)
    c_t = i_t * c_cand + f_t * f64(c_state)
    h_t = o_t * np.tanh(c_t)
    return (h_t, c_t)

@@ -1,0 +1,309 @@
+from contextlib import ExitStack
+
+import concourse.masks as masks
+import concourse.mybir as mybir
+
+BF16 = mybir.dt.bfloat16
+F32 = mybir.dt.float32
+U32 = mybir.dt.uint32
+U8 = mybir.dt.uint8
+FP8X4 = mybir.dt.float8_e4m3fn_x4
+ACT = mybir.ActivationFunctionType
+ALU = mybir.AluOpType
+
+P = 128
+BATCH = 256
+K = 1024
+HIDDEN = 1024
+B_TILES = BATCH // P
+PACK = 4
+PASSES = K // (P * PACK)
+WORDS = K // 2
+BANK = 512
+CHUNK = BANK
+ROWS = CHUNK // P
+HALVES = HIDDEN // CHUNK
+
+FLOPS = 2 * BATCH * K * 4 * HIDDEN * 4
+
+GATE_I, GATE_F, GATE_O, GATE_C = 0, 1, 2, 3
+GATE_ORDER = (GATE_F, GATE_I, GATE_C, GATE_O)
+
+PREFETCH = 8
+
+
+def tile_scncore_pa_kernel(
+    tc, core_input, h_state, c_state, concept, W_in, W_st, W_ci, W_cs, out_0, out_1
+):
+    nc = tc.nc
+    weights = (W_ci, W_in, W_cs, W_st)
+    operands = (concept, core_input, concept, h_state)
+    operand_names = ("concept", "core_input", "concept", "h_state")
+    chunks = [
+        (half, gate, m)
+        for half in range(HALVES)
+        for gate in GATE_ORDER
+        for m in range(len(weights))
+    ]
+    n_chunks = len(chunks)
+    h_view = out_0.rearrange("(p b) h -> p b h", b=B_TILES)
+    c_view = out_1.rearrange("(p b) h -> p b h", b=B_TILES)
+
+    with ExitStack() as ctx:
+        const = ctx.enter_context(tc.tile_pool(name="const", bufs=1))
+        act_pool = ctx.enter_context(tc.tile_pool(name="activations", bufs=1))
+        w_pool = ctx.enter_context(tc.tile_pool(name="w_raw", bufs=PREFETCH))
+        grouped_pool = ctx.enter_context(tc.tile_pool(name="grouped", bufs=3))
+        code_pool = ctx.enter_context(tc.tile_pool(name="codes", bufs=4))
+        gate_pool = ctx.enter_context(tc.tile_pool(name="gate", bufs=2))
+        hidden_pool = ctx.enter_context(tc.tile_pool(name="hidden", bufs=3))
+        cell_pool = ctx.enter_context(tc.tile_pool(name="cell", bufs=1))
+        turn_pool = ctx.enter_context(tc.psum_pool(name="turned", bufs=5))
+        acc_pool = ctx.enter_context(tc.psum_pool(name="acc", bufs=3))
+
+        identity = const.tile([P, P], F32, name="identity")
+        masks.make_identity(nc, identity[:])
+
+        x_raw = {}
+        x_mx = {}
+        w_raw = {}
+        w_grouped = {}
+        w_mx = {}
+        modulator = {}
+        product = {}
+        pre = {}
+        hidden = {}
+        cell = {}
+
+        def load_operand(m):
+            if operand_names[m] in x_raw:
+                return
+            raw = act_pool.tile([P, B_TILES * K], BF16, name=operand_names[m] + "_raw")
+            nc.sync.dma_start(
+                out=raw[:], in_=operands[m].rearrange("(p b) k -> p (b k)", b=B_TILES)
+            )
+            x_raw[operand_names[m]] = raw
+
+        def load_chunk(j):
+            if j >= n_chunks:
+                return
+            half, gate, m = chunks[j]
+            row0 = gate * HIDDEN + half * CHUNK
+            raw = w_pool.tile([P, ROWS * K], BF16, name="w_raw")
+            nc.sync.dma_start(
+                out=raw[:],
+                in_=weights[m][row0 : row0 + CHUNK, :].rearrange("(c r) k -> c (r k)", r=ROWS),
+            )
+            w_raw[j] = raw
+
+        def quantise_operand(m):
+            name = operand_names[m]
+            if name in x_mx:
+                return
+            words = x_raw[name][:].bitcast(F32)
+            grouped = act_pool.tile(
+                [P, PASSES * BATCH * PACK], BF16, name=name + "_grouped", align_bytes=64
+            )
+            grouped_words = grouped[:].bitcast(F32).rearrange("p (s n) -> p s n", s=PASSES)
+            for s in range(PASSES):
+                bank = turn_pool.tile([P, BANK], F32, name="bank")
+                for b in range(B_TILES):
+                    for u in range(2):
+                        col = b * WORDS + 2 * s * P
+                        slot = (2 * b + u) * P
+                        nc.tensor.transpose(
+                            bank[:, slot : slot + P],
+                            words[:, col + u : col + 2 * P : 2],
+                            identity[:],
+                        )
+                nc.scalar.copy(
+                    out=grouped_words[:, s, :].rearrange("p (b c u) -> p b c u", b=B_TILES, u=2),
+                    in_=bank[:].rearrange("p (b u c) -> p b c u", b=B_TILES, u=2),
+                )
+            codes = act_pool.tile([P, PASSES * BATCH], U32, name=name + "_codes", align_bytes=64)
+            scales = act_pool.tile([P, PASSES * BATCH], U8, name=name + "_scales", align_bytes=64)
+            nc.vector.quantize_mx(out=codes[:].bitcast(FP8X4), scales=scales[:], in_=grouped[:])
+            x_mx[name] = (codes, scales)
+
+        def transpose_pass(j, s):
+            if j >= n_chunks:
+                return
+            words = w_raw[j][:].bitcast(F32)
+            if s == 0:
+                w_grouped[j] = grouped_pool.tile(
+                    [P, PASSES * CHUNK * PACK], BF16, name="w_grouped", align_bytes=64
+                )
+            grouped_words = w_grouped[j][:].bitcast(F32).rearrange(
+                "p (s c rh q) -> p s c rh q", s=PASSES, c=P, rh=2
+            )
+            for rh in range(2):
+                bank = turn_pool.tile([P, BANK], F32, name="bank")
+                for rl in range(2):
+                    for u in range(2):
+                        col = (2 * rh + rl) * WORDS + 2 * s * P
+                        slot = (2 * rl + u) * P
+                        nc.tensor.transpose(
+                            bank[:, slot : slot + P],
+                            words[:, col + u : col + 2 * P : 2],
+                            identity[:],
+                        )
+                nc.scalar.copy(
+                    out=grouped_words[:, s, :, rh, :],
+                    in_=bank[:].rearrange("p (q c) -> p c q", c=P),
+                )
+
+        def quantise_chunk(j):
+            if not 0 <= j < n_chunks:
+                return
+            codes = code_pool.tile([P, PASSES * CHUNK], U32, name="w_codes", align_bytes=64)
+            scales = code_pool.tile([P, PASSES * CHUNK], U8, name="w_scales", align_bytes=64)
+            for s in range(PASSES):
+                cols = slice(s * CHUNK, (s + 1) * CHUNK)
+                nc.vector.quantize_mx(
+                    out=codes[:, cols].bitcast(FP8X4),
+                    scales=scales[:, cols],
+                    in_=w_grouped[j][:, s * CHUNK * PACK : (s + 1) * CHUNK * PACK],
+                )
+            w_mx[j] = (codes, scales)
+
+        def multiply_tile(j, b):
+            if not 0 <= j < n_chunks:
+                return
+            m = chunks[j][2]
+            x_codes, x_scales = x_mx[operand_names[m]]
+            w_codes, w_scales = w_mx[j]
+            modulates = m % 2 == 0
+            if modulates and b == 0:
+                modulator[j] = gate_pool.tile([P, B_TILES, CHUNK], F32, name="modulator")
+            if not modulates and b == 0:
+                product[j] = gate_pool.tile([P, B_TILES, CHUNK], F32, name="product%d" % m)
+            acc = acc_pool.tile([P, CHUNK], F32, name="acc")
+            for s in range(PASSES):
+                x_cols = slice((s * B_TILES + b) * P, (s * B_TILES + b + 1) * P)
+                w_cols = slice(s * CHUNK, (s + 1) * CHUNK)
+                nc.tensor.matmul_mx(
+                    out=acc[:],
+                    lhsT=x_codes[:, x_cols].bitcast(FP8X4),
+                    lhsT_scale=x_scales[:, x_cols],
+                    rhs=w_codes[:, w_cols].bitcast(FP8X4),
+                    rhs_scale=w_scales[:, w_cols],
+                    start=(s == 0),
+                    stop=(s == PASSES - 1),
+                )
+            if modulates:
+                nc.vector.tensor_copy(out=modulator[j][:, b, :], in_=acc[:])
+            else:
+                nc.vector.tensor_tensor(
+                    out=product[j][:, b, :],
+                    in0=acc[:],
+                    in1=modulator[j - 1][:, b, :],
+                    op=ALU.mult,
+                )
+
+        def closes_gate(j):
+            return 0 <= j < n_chunks and chunks[j][2] == len(weights) - 1
+
+        def worker(j):
+            return nc.vector if j == n_chunks - 1 else nc.gpsimd
+
+        def add_products(j, b):
+            if not closes_gate(j):
+                return
+            if b == 0:
+                pre[j] = gate_pool.tile([P, B_TILES, CHUNK], F32, name="pre")
+            worker(j).tensor_tensor(
+                out=pre[j][:, b, :],
+                in0=product[j - 2][:, b, :],
+                in1=product[j][:, b, :],
+                op=ALU.add,
+            )
+
+        def squash_gate(j, b):
+            if not closes_gate(j):
+                return
+            half, gate = chunks[j][0], chunks[j][1]
+            if b == 0:
+                hidden[half, gate] = hidden_pool.tile([P, B_TILES, CHUNK], F32, name="hidden")
+            nc.scalar.activation(
+                out=hidden[half, gate][:, b, :], in_=pre[j][:, b, :], func=ACT.Sigmoid
+            )
+
+        def update_cell(j, b):
+            if not closes_gate(j):
+                return
+            half, gate = chunks[j][0], chunks[j][1]
+            cols = slice(half * CHUNK, (half + 1) * CHUNK)
+            if gate == GATE_F:
+                if b == 0:
+                    cell[half, "kept"] = cell_pool.tile([P, B_TILES, CHUNK], F32, name="kept")
+                worker(j).tensor_tensor(
+                    out=cell[half, "kept"][:, b, :],
+                    in0=hidden[half, GATE_F][:, b, :],
+                    in1=c_prev[:, b, cols],
+                    op=ALU.mult,
+                )
+            if gate == GATE_C:
+                if b == 0:
+                    cell[half, "fresh"] = cell_pool.tile([P, B_TILES, CHUNK], F32, name="fresh")
+                    cell[half, "c_new"] = cell_pool.tile([P, B_TILES, CHUNK], F32, name="c_new")
+                worker(j).tensor_tensor(
+                    out=cell[half, "fresh"][:, b, :],
+                    in0=hidden[half, GATE_I][:, b, :],
+                    in1=hidden[half, GATE_C][:, b, :],
+                    op=ALU.mult,
+                )
+                worker(j).tensor_tensor(
+                    out=cell[half, "c_new"][:, b, :],
+                    in0=cell[half, "fresh"][:, b, :],
+                    in1=cell[half, "kept"][:, b, :],
+                    op=ALU.add,
+                )
+                nc.sync.dma_start(out=c_view[:, b, cols], in_=cell[half, "c_new"][:, b, :])
+            if gate == GATE_O:
+                if b == 0:
+                    cell[half, "h_new"] = cell_pool.tile([P, B_TILES, CHUNK], F32, name="h_new")
+                worker(j).tensor_tensor(
+                    out=cell[half, "h_new"][:, b, :],
+                    in0=hidden[half, GATE_O][:, b, :],
+                    in1=cell[half, "tanh_c"][:, b, :],
+                    op=ALU.mult,
+                )
+                nc.sync.dma_start(out=h_view[:, b, cols], in_=cell[half, "h_new"][:, b, :])
+
+        def squash_cell(j, b):
+            if not closes_gate(j) or chunks[j][1] != GATE_C:
+                return
+            half = chunks[j][0]
+            if b == 0:
+                cell[half, "tanh_c"] = cell_pool.tile([P, B_TILES, CHUNK], F32, name="tanh_c")
+            nc.scalar.activation(
+                out=cell[half, "tanh_c"][:, b, :], in_=cell[half, "c_new"][:, b, :], func=ACT.Tanh
+            )
+
+        ctx.enter_context(tc.manual_schedule())
+
+        for j in range(len(weights)):
+            load_operand(j)
+            load_chunk(j)
+        c_prev = act_pool.tile([P, B_TILES, HIDDEN], BF16, name="c_prev")
+        nc.sync.dma_start(out=c_prev[:], in_=c_state.rearrange("(p b) h -> p b h", b=B_TILES))
+        for j in range(len(weights), PREFETCH):
+            load_chunk(j)
+
+        for step in range(n_chunks + 9):
+            add_products(step - 3, 0)
+            add_products(step - 3, 1)
+            if step < len(weights):
+                quantise_operand(step)
+            transpose_pass(step, 0)
+            quantise_chunk(step - 1)
+            multiply_tile(step - 2, 0)
+            transpose_pass(step, 1)
+            load_chunk(step + PREFETCH)
+            squash_gate(step - 4, 0)
+            squash_gate(step - 5, 1)
+            squash_cell(step - 7, 0)
+            squash_cell(step - 8, 1)
+            multiply_tile(step - 2, 1)
+            update_cell(step - 5, 0)
+            update_cell(step - 6, 1)

@@ -30,6 +30,7 @@ GATE_I, GATE_F, GATE_O, GATE_C = 0, 1, 2, 3
 GATE_ORDER = (GATE_F, GATE_I, GATE_C, GATE_O)
 
 PREFETCH = 8
+SORTED = 2
 
 
 def tile_scncore_pa_kernel(
@@ -53,6 +54,7 @@ def tile_scncore_pa_kernel(
         const = ctx.enter_context(tc.tile_pool(name="const", bufs=1))
         act_pool = ctx.enter_context(tc.tile_pool(name="activations", bufs=1))
         w_pool = ctx.enter_context(tc.tile_pool(name="w_raw", bufs=PREFETCH))
+        sorted_pool = ctx.enter_context(tc.tile_pool(name="sorted", bufs=3))
         grouped_pool = ctx.enter_context(tc.tile_pool(name="grouped", bufs=3))
         code_pool = ctx.enter_context(tc.tile_pool(name="codes", bufs=4))
         gate_pool = ctx.enter_context(tc.tile_pool(name="gate", bufs=2))
@@ -66,6 +68,7 @@ def tile_scncore_pa_kernel(
 
         x_raw = {}
         x_mx = {}
+        w_sorted = {}
         w_raw = {}
         w_grouped = {}
         w_mx = {}
@@ -125,10 +128,22 @@ def tile_scncore_pa_kernel(
             nc.vector.quantize_mx(out=codes[:].bitcast(FP8X4), scales=scales[:], in_=grouped[:])
             x_mx[name] = (codes, scales)
 
+        def sort_chunk(j):
+            if not 0 <= j < n_chunks:
+                return
+            w_sorted[j] = sorted_pool.tile([P, SORTED * K], BF16, name="w_sorted")
+            nc.vector.tensor_copy(
+                out=w_sorted[j][:].bitcast(F32).rearrange("p (g u q) -> p g u q", u=2, q=P),
+                in_=w_raw[j][:, : SORTED * K]
+                .bitcast(F32)
+                .rearrange("p (g q u) -> p g u q", u=2, q=P),
+            )
+
         def transpose_pass(j, s):
             if j >= n_chunks:
                 return
             words = w_raw[j][:].bitcast(F32)
+            sorted_words = w_sorted[j][:].bitcast(F32)
             if s == 0:
                 w_grouped[j] = grouped_pool.tile(
                     [P, PASSES * CHUNK * PACK], BF16, name="w_grouped", align_bytes=64
@@ -140,13 +155,14 @@ def tile_scncore_pa_kernel(
                 bank = turn_pool.tile([P, BANK], F32, name="bank")
                 for rl in range(2):
                     for u in range(2):
-                        col = (2 * rh + rl) * WORDS + 2 * s * P
+                        r = 2 * rh + rl
+                        col = r * WORDS + 2 * s * P
                         slot = (2 * rl + u) * P
-                        nc.tensor.transpose(
-                            bank[:, slot : slot + P],
-                            words[:, col + u : col + 2 * P : 2],
-                            identity[:],
-                        )
+                        if r < SORTED:
+                            block = sorted_words[:, col + u * P : col + (u + 1) * P]
+                        else:
+                            block = words[:, col + u : col + 2 * P : 2]
+                        nc.tensor.transpose(bank[:, slot : slot + P], block, identity[:])
                 nc.scalar.copy(
                     out=grouped_words[:, s, :, rh, :],
                     in_=bank[:].rearrange("p (q c) -> p c q", c=P),
@@ -290,6 +306,7 @@ def tile_scncore_pa_kernel(
         for j in range(len(weights), PREFETCH):
             load_chunk(j)
 
+        sort_chunk(0)
         for step in range(n_chunks + 9):
             add_products(step - 3, 0)
             add_products(step - 3, 1)
@@ -298,6 +315,7 @@ def tile_scncore_pa_kernel(
             transpose_pass(step, 0)
             quantise_chunk(step - 1)
             multiply_tile(step - 2, 0)
+            sort_chunk(step + 1)
             transpose_pass(step, 1)
             load_chunk(step + PREFETCH)
             squash_gate(step - 4, 0)

@@ -30,7 +30,26 @@ GATE_I, GATE_F, GATE_O, GATE_C = 0, 1, 2, 3
 GATE_ORDER = (GATE_F, GATE_I, GATE_C, GATE_O)
 
 PREFETCH = 8
+TURN_BANKS = 5
 SORTED = 2
+AHEAD = 2
+SORT_FROM = 3
+UNSORTED_TAIL = 0
+LAST_S = 4
+MUL = 2
+FIRST_PIECES = 2
+PIECED = 4
+CPREV_AT = 6
+ORDER = (0, 1, 2, 3)
+FIRST_ORDER = (0, 1, 2, 3)
+XV = False
+XQLATE = False
+LASTV = False
+GI_SCALAR = ((0, 0), (2, 0))
+ADD_G = False
+CELL_G = False
+GW = 256
+ADD0, ADD1, SIG0, SIG1, CELL0, CELL1, TANH0, TANH1 = 3, 3, 4, 4, 5, 5, 6, 6
 
 
 def tile_scncore_pa_kernel(
@@ -44,7 +63,7 @@ def tile_scncore_pa_kernel(
         (half, gate, m)
         for half in range(HALVES)
         for gate in GATE_ORDER
-        for m in range(len(weights))
+        for m in (FIRST_ORDER if half == 0 and gate == GATE_ORDER[0] else ORDER)
     ]
     n_chunks = len(chunks)
     h_view = out_0.rearrange("(p b) h -> p b h", b=B_TILES)
@@ -54,24 +73,25 @@ def tile_scncore_pa_kernel(
         const = ctx.enter_context(tc.tile_pool(name="const", bufs=1))
         act_pool = ctx.enter_context(tc.tile_pool(name="activations", bufs=1))
         w_pool = ctx.enter_context(tc.tile_pool(name="w_raw", bufs=PREFETCH))
-        sorted_pool = ctx.enter_context(tc.tile_pool(name="sorted", bufs=3))
+        sorted_pool = ctx.enter_context(tc.tile_pool(name="sorted", bufs=AHEAD + 2))
         grouped_pool = ctx.enter_context(tc.tile_pool(name="grouped", bufs=3))
         code_pool = ctx.enter_context(tc.tile_pool(name="codes", bufs=4))
         gate_pool = ctx.enter_context(tc.tile_pool(name="gate", bufs=2))
         hidden_pool = ctx.enter_context(tc.tile_pool(name="hidden", bufs=3))
         cell_pool = ctx.enter_context(tc.tile_pool(name="cell", bufs=1))
-        turn_pool = ctx.enter_context(tc.psum_pool(name="turned", bufs=5))
-        acc_pool = ctx.enter_context(tc.psum_pool(name="acc", bufs=3))
+        turn_pool = ctx.enter_context(tc.psum_pool(name="turned", bufs=TURN_BANKS))
+        acc_pool = ctx.enter_context(tc.psum_pool(name="acc", bufs=8 - TURN_BANKS))
 
         identity = const.tile([P, P], F32, name="identity")
         masks.make_identity(nc, identity[:])
 
         x_raw = {}
         x_mx = {}
-        w_sorted = {}
         w_raw = {}
+        w_sorted = {}
         w_grouped = {}
         w_mx = {}
+        acc_of = {}
         modulator = {}
         product = {}
         pre = {}
@@ -82,9 +102,11 @@ def tile_scncore_pa_kernel(
             if operand_names[m] in x_raw:
                 return
             raw = act_pool.tile([P, B_TILES * K], BF16, name=operand_names[m] + "_raw")
-            nc.sync.dma_start(
-                out=raw[:], in_=operands[m].rearrange("(p b) k -> p (b k)", b=B_TILES)
-            )
+            view = operands[m].rearrange("(p b) k -> p (b k)", b=B_TILES)
+            pieces = B_TILES if m == 0 else 1
+            n = B_TILES * K // pieces
+            for i in range(pieces):
+                nc.sync.dma_start(out=raw[:, i * n : (i + 1) * n], in_=view[:, i * n : (i + 1) * n])
             x_raw[operand_names[m]] = raw
 
         def load_chunk(j):
@@ -93,13 +115,14 @@ def tile_scncore_pa_kernel(
             half, gate, m = chunks[j]
             row0 = gate * HIDDEN + half * CHUNK
             raw = w_pool.tile([P, ROWS * K], BF16, name="w_raw")
-            nc.sync.dma_start(
-                out=raw[:],
-                in_=weights[m][row0 : row0 + CHUNK, :].rearrange("(c r) k -> c (r k)", r=ROWS),
-            )
+            view = weights[m][row0 : row0 + CHUNK, :].rearrange("(c r) k -> c (r k)", r=ROWS)
+            pieces = FIRST_PIECES if j < PIECED else 1
+            n = ROWS * K // pieces
+            for i in range(pieces):
+                nc.sync.dma_start(out=raw[:, i * n : (i + 1) * n], in_=view[:, i * n : (i + 1) * n])
             w_raw[j] = raw
 
-        def quantise_operand(m):
+        def turn_operand(m):
             name = operand_names[m]
             if name in x_mx:
                 return
@@ -119,17 +142,21 @@ def tile_scncore_pa_kernel(
                             words[:, col + u : col + 2 * P : 2],
                             identity[:],
                         )
-                nc.scalar.copy(
+                (nc.vector.tensor_copy if XV else nc.scalar.copy)(
                     out=grouped_words[:, s, :].rearrange("p (b c u) -> p b c u", b=B_TILES, u=2),
                     in_=bank[:].rearrange("p (b u c) -> p b c u", b=B_TILES, u=2),
                 )
             codes = act_pool.tile([P, PASSES * BATCH], U32, name=name + "_codes", align_bytes=64)
             scales = act_pool.tile([P, PASSES * BATCH], U8, name=name + "_scales", align_bytes=64)
+            x_mx[name] = (codes, scales, grouped)
+
+        def quantise_operand(m):
+            name = operand_names[m]
+            codes, scales, grouped = x_mx[name]
             nc.vector.quantize_mx(out=codes[:].bitcast(FP8X4), scales=scales[:], in_=grouped[:])
-            x_mx[name] = (codes, scales)
 
         def sort_chunk(j):
-            if not 0 <= j < n_chunks:
+            if not SORT_FROM <= j < n_chunks - UNSORTED_TAIL or SORTED == 0:
                 return
             w_sorted[j] = sorted_pool.tile([P, SORTED * K], BF16, name="w_sorted")
             nc.vector.tensor_copy(
@@ -139,61 +166,56 @@ def tile_scncore_pa_kernel(
                 .rearrange("p (g q u) -> p g u q", u=2, q=P),
             )
 
-        def transpose_pass(j, s):
+        def turn_bank(j, s, rh):
             if j >= n_chunks:
                 return
             words = w_raw[j][:].bitcast(F32)
-            sorted_words = w_sorted[j][:].bitcast(F32)
-            if s == 0:
+            if s == 0 and rh == 0:
                 w_grouped[j] = grouped_pool.tile(
                     [P, PASSES * CHUNK * PACK], BF16, name="w_grouped", align_bytes=64
                 )
             grouped_words = w_grouped[j][:].bitcast(F32).rearrange(
                 "p (s c rh q) -> p s c rh q", s=PASSES, c=P, rh=2
             )
-            for rh in range(2):
-                bank = turn_pool.tile([P, BANK], F32, name="bank")
-                for rl in range(2):
-                    for u in range(2):
-                        r = 2 * rh + rl
-                        col = r * WORDS + 2 * s * P
-                        slot = (2 * rl + u) * P
-                        if r < SORTED:
-                            block = sorted_words[:, col + u * P : col + (u + 1) * P]
-                        else:
-                            block = words[:, col + u : col + 2 * P : 2]
-                        nc.tensor.transpose(bank[:, slot : slot + P], block, identity[:])
-                nc.scalar.copy(
-                    out=grouped_words[:, s, :, rh, :],
-                    in_=bank[:].rearrange("p (q c) -> p c q", c=P),
-                )
+            bank = turn_pool.tile([P, BANK], F32, name="bank")
+            for rl in range(2):
+                for u in range(2):
+                    r = 2 * rh + rl
+                    col = r * WORDS + 2 * s * P
+                    slot = (2 * rl + u) * P
+                    if r < SORTED and SORT_FROM <= j < n_chunks - UNSORTED_TAIL:
+                        block = w_sorted[j][:].bitcast(F32)[:, col + u * P : col + (u + 1) * P]
+                    else:
+                        block = words[:, col + u : col + 2 * P : 2]
+                    nc.tensor.transpose(bank[:, slot : slot + P], block, identity[:])
+            vec = LASTV and j == n_chunks - 1 and s == 1
+            (nc.vector.tensor_copy if vec else nc.scalar.copy)(
+                out=grouped_words[:, s, :, rh, :],
+                in_=bank[:].rearrange("p (q c) -> p c q", c=P),
+            )
 
-        def quantise_chunk(j):
+        def quantise_pass(j, s):
             if not 0 <= j < n_chunks:
                 return
-            codes = code_pool.tile([P, PASSES * CHUNK], U32, name="w_codes", align_bytes=64)
-            scales = code_pool.tile([P, PASSES * CHUNK], U8, name="w_scales", align_bytes=64)
-            for s in range(PASSES):
-                cols = slice(s * CHUNK, (s + 1) * CHUNK)
-                nc.vector.quantize_mx(
-                    out=codes[:, cols].bitcast(FP8X4),
-                    scales=scales[:, cols],
-                    in_=w_grouped[j][:, s * CHUNK * PACK : (s + 1) * CHUNK * PACK],
-                )
-            w_mx[j] = (codes, scales)
+            if s == 0:
+                codes = code_pool.tile([P, PASSES * CHUNK], U32, name="w_codes", align_bytes=64)
+                scales = code_pool.tile([P, PASSES * CHUNK], U8, name="w_scales", align_bytes=64)
+                w_mx[j] = (codes, scales)
+            codes, scales = w_mx[j]
+            cols = slice(s * CHUNK, (s + 1) * CHUNK)
+            nc.vector.quantize_mx(
+                out=codes[:, cols].bitcast(FP8X4),
+                scales=scales[:, cols],
+                in_=w_grouped[j][:, s * CHUNK * PACK : (s + 1) * CHUNK * PACK],
+            )
 
         def multiply_tile(j, b):
             if not 0 <= j < n_chunks:
                 return
-            m = chunks[j][2]
-            x_codes, x_scales = x_mx[operand_names[m]]
+            x_codes, x_scales, x_grouped = x_mx[operand_names[chunks[j][2]]]
             w_codes, w_scales = w_mx[j]
-            modulates = m % 2 == 0
-            if modulates and b == 0:
-                modulator[j] = gate_pool.tile([P, B_TILES, CHUNK], F32, name="modulator")
-            if not modulates and b == 0:
-                product[j] = gate_pool.tile([P, B_TILES, CHUNK], F32, name="product%d" % m)
             acc = acc_pool.tile([P, CHUNK], F32, name="acc")
+            acc_of[j, b] = acc
             for s in range(PASSES):
                 x_cols = slice((s * B_TILES + b) * P, (s * B_TILES + b + 1) * P)
                 w_cols = slice(s * CHUNK, (s + 1) * CHUNK)
@@ -206,33 +228,52 @@ def tile_scncore_pa_kernel(
                     start=(s == 0),
                     stop=(s == PASSES - 1),
                 )
-            if modulates:
-                nc.vector.tensor_copy(out=modulator[j][:, b, :], in_=acc[:])
+
+        def drain_tile(j, b):
+            if not 0 <= j < n_chunks:
+                return
+            m = chunks[j][2]
+            acc = acc_of[j, b]
+            if m % 2 == 0:
+                if b == 0:
+                    modulator[half_gate(j) + (m,)] = gate_pool.tile([P, B_TILES, CHUNK], F32, name="modulator", bufs=3)
+                copy = nc.scalar.copy if (m, b) in GI_SCALAR or j >= n_chunks - LAST_S else nc.vector.tensor_copy
+                copy(out=modulator[half_gate(j) + (m,)][:, b, :], in_=acc[:])
             else:
+                if b == 0:
+                    product[half_gate(j) + (m,)] = gate_pool.tile([P, B_TILES, CHUNK], F32, name="product%d" % m)
                 nc.vector.tensor_tensor(
-                    out=product[j][:, b, :],
+                    out=product[half_gate(j) + (m,)][:, b, :],
                     in0=acc[:],
-                    in1=modulator[j - 1][:, b, :],
+                    in1=modulator[half_gate(j) + (m - 1,)][:, b, :],
                     op=ALU.mult,
                 )
+
+        def half_gate(j):
+            return chunks[j][:2]
 
         def closes_gate(j):
             return 0 <= j < n_chunks and chunks[j][2] == len(weights) - 1
 
         def worker(j):
-            return nc.vector if j == n_chunks - 1 else nc.gpsimd
+            return nc.gpsimd if ADD_G and j < n_chunks - 1 else nc.vector
+
+        def cworker(j):
+            return nc.gpsimd if CELL_G and j < n_chunks - 1 else nc.vector
 
         def add_products(j, b):
             if not closes_gate(j):
                 return
             if b == 0:
                 pre[j] = gate_pool.tile([P, B_TILES, CHUNK], F32, name="pre")
-            worker(j).tensor_tensor(
-                out=pre[j][:, b, :],
-                in0=product[j - 2][:, b, :],
-                in1=product[j][:, b, :],
-                op=ALU.add,
-            )
+            for c0 in range(0, CHUNK, GW if worker(j) is nc.gpsimd else CHUNK):
+                c1 = c0 + (GW if worker(j) is nc.gpsimd else CHUNK)
+                worker(j).tensor_tensor(
+                    out=pre[j][:, b, c0:c1],
+                    in0=product[half_gate(j) + (1,)][:, b, c0:c1],
+                    in1=product[half_gate(j) + (3,)][:, b, c0:c1],
+                    op=ALU.add,
+                )
 
         def squash_gate(j, b):
             if not closes_gate(j):
@@ -244,6 +285,12 @@ def tile_scncore_pa_kernel(
                 out=hidden[half, gate][:, b, :], in_=pre[j][:, b, :], func=ACT.Sigmoid
             )
 
+        def two(j, out, in0, in1, op):
+            w = cworker(j)
+            n = GW if w is nc.gpsimd else CHUNK
+            for c0 in range(0, CHUNK, n):
+                w.tensor_tensor(out=out[:, c0:c0+n], in0=in0[:, c0:c0+n], in1=in1[:, c0:c0+n], op=op)
+
         def update_cell(j, b):
             if not closes_gate(j):
                 return
@@ -252,39 +299,25 @@ def tile_scncore_pa_kernel(
             if gate == GATE_F:
                 if b == 0:
                     cell[half, "kept"] = cell_pool.tile([P, B_TILES, CHUNK], F32, name="kept")
-                worker(j).tensor_tensor(
-                    out=cell[half, "kept"][:, b, :],
-                    in0=hidden[half, GATE_F][:, b, :],
-                    in1=c_prev[:, b, cols],
-                    op=ALU.mult,
-                )
+                two(j, cell[half, "kept"][:, b, :], hidden[half, GATE_F][:, b, :], c_prev[:, b, cols], ALU.mult)
             if gate == GATE_C:
                 if b == 0:
                     cell[half, "fresh"] = cell_pool.tile([P, B_TILES, CHUNK], F32, name="fresh")
                     cell[half, "c_new"] = cell_pool.tile([P, B_TILES, CHUNK], F32, name="c_new")
-                worker(j).tensor_tensor(
-                    out=cell[half, "fresh"][:, b, :],
-                    in0=hidden[half, GATE_I][:, b, :],
-                    in1=hidden[half, GATE_C][:, b, :],
-                    op=ALU.mult,
-                )
-                worker(j).tensor_tensor(
-                    out=cell[half, "c_new"][:, b, :],
-                    in0=cell[half, "fresh"][:, b, :],
-                    in1=cell[half, "kept"][:, b, :],
-                    op=ALU.add,
-                )
-                nc.sync.dma_start(out=c_view[:, b, cols], in_=cell[half, "c_new"][:, b, :])
+                two(j, cell[half, "fresh"][:, b, :], hidden[half, GATE_I][:, b, :], hidden[half, GATE_C][:, b, :], ALU.mult)
             if gate == GATE_O:
                 if b == 0:
                     cell[half, "h_new"] = cell_pool.tile([P, B_TILES, CHUNK], F32, name="h_new")
-                worker(j).tensor_tensor(
-                    out=cell[half, "h_new"][:, b, :],
-                    in0=hidden[half, GATE_O][:, b, :],
-                    in1=cell[half, "tanh_c"][:, b, :],
-                    op=ALU.mult,
-                )
+                two(j, cell[half, "h_new"][:, b, :], hidden[half, GATE_O][:, b, :], cell[half, "tanh_c"][:, b, :], ALU.mult)
                 nc.sync.dma_start(out=h_view[:, b, cols], in_=cell[half, "h_new"][:, b, :])
+
+        def update_cell2(j, b):
+            if not closes_gate(j) or chunks[j][1] != GATE_C:
+                return
+            half = chunks[j][0]
+            cols = slice(half * CHUNK, (half + 1) * CHUNK)
+            two(j, cell[half, "c_new"][:, b, :], cell[half, "fresh"][:, b, :], cell[half, "kept"][:, b, :], ALU.add)
+            nc.sync.dma_start(out=c_view[:, b, cols], in_=cell[half, "c_new"][:, b, :])
 
         def squash_cell(j, b):
             if not closes_gate(j) or chunks[j][1] != GATE_C:
@@ -297,31 +330,45 @@ def tile_scncore_pa_kernel(
             )
 
         ctx.enter_context(tc.manual_schedule())
-
-        for j in range(len(weights)):
-            load_operand(j)
-            load_chunk(j)
         c_prev = act_pool.tile([P, B_TILES, HIDDEN], BF16, name="c_prev")
-        nc.sync.dma_start(out=c_prev[:], in_=c_state.rearrange("(p b) h -> p b h", b=B_TILES))
-        for j in range(len(weights), PREFETCH):
+        for j in range(PREFETCH):
+            if j == CPREV_AT:
+                nc.sync.dma_start(out=c_prev[:], in_=c_state.rearrange("(p b) h -> p b h", b=B_TILES))
+            if j < 4:
+                load_operand(chunks[j][2])
             load_chunk(j)
-
-        sort_chunk(0)
+        for j in range(AHEAD):
+            if j == 0:
+                sort_chunk(j)
         for step in range(n_chunks + 9):
-            add_products(step - 3, 0)
-            add_products(step - 3, 1)
-            if step < len(weights):
+            n = step
+            if step < len(weights) and operand_names[chunks[step][2]] not in x_mx:
+                turn_operand(chunks[step][2])
+                if not XQLATE:
+                    quantise_operand(chunks[step][2])
+            if 0 < step < AHEAD:
+                sort_chunk(step)
+            turn_bank(n, 0, 0)
+            turn_bank(n, 0, 1)
+            quantise_pass(n - 1, 0)
+            multiply_tile(n - MUL, 0)
+            drain_tile(n - MUL, 0)
+            add_products(n - ADD0, 0)
+            add_products(n - ADD1, 1)
+            squash_gate(n - SIG0, 0)
+            turn_bank(n, 1, 0)
+            turn_bank(n, 1, 1)
+            squash_gate(n - SIG1, 1)
+            squash_cell(n - TANH0, 0)
+            squash_cell(n - TANH1, 1)
+            load_chunk(n + PREFETCH)
+            quantise_pass(n - 1, 1)
+            sort_chunk(n + AHEAD)
+            multiply_tile(n - MUL, 1)
+            drain_tile(n - MUL, 1)
+            if XQLATE and step in (0, 1, 3):
                 quantise_operand(step)
-            transpose_pass(step, 0)
-            quantise_chunk(step - 1)
-            multiply_tile(step - 2, 0)
-            sort_chunk(step + 1)
-            transpose_pass(step, 1)
-            load_chunk(step + PREFETCH)
-            squash_gate(step - 4, 0)
-            squash_gate(step - 5, 1)
-            squash_cell(step - 7, 0)
-            squash_cell(step - 8, 1)
-            multiply_tile(step - 2, 1)
-            update_cell(step - 5, 0)
-            update_cell(step - 6, 1)
+            update_cell(n - CELL0, 0)
+            update_cell(n - CELL1, 1)
+            update_cell2(n - CELL0, 0)
+            update_cell2(n - CELL1, 1)

@@ -31,7 +31,7 @@ GATE_ORDER = (GATE_F, GATE_I, GATE_C, GATE_O)
 
 PREFETCH = 8
 TURN_BANKS = 5
-SORTED = 2
+SORTED = 0
 AHEAD = 2
 SORT_FROM = 3
 UNSORTED_TAIL = 0

from contextlib import ExitStack

import concourse.masks as masks
import concourse.mybir as mybir

BF16 = mybir.dt.bfloat16
F32 = mybir.dt.float32
U32 = mybir.dt.uint32
U8 = mybir.dt.uint8
FP8X4 = mybir.dt.float8_e4m3fn_x4
ACT = mybir.ActivationFunctionType
ALU = mybir.AluOpType

P = 128
BATCH = 256
K = 1024
HIDDEN = 1024
B_TILES = BATCH // P
PACK = 4
PASSES = K // (P * PACK)
WORDS = K // 2
BANK = 512
CHUNK = BANK
ROWS = CHUNK // P
HALVES = HIDDEN // CHUNK

FLOPS = 2 * BATCH * K * 4 * HIDDEN * 4

GATE_I, GATE_F, GATE_O, GATE_C = 0, 1, 2, 3
GATE_ORDER = (GATE_F, GATE_I, GATE_C, GATE_O)

PREFETCH = 8
TURN_BANKS = 5
SORTED = 0
AHEAD = 2
SORT_FROM = 3
UNSORTED_TAIL = 0
LAST_S = 4
MUL = 2
FIRST_PIECES = 2
PIECED = 4
CPREV_AT = 6
ORDER = (0, 1, 2, 3)
FIRST_ORDER = (0, 1, 2, 3)
XV = False
XQLATE = False
LASTV = False
GI_SCALAR = ((0, 0), (2, 0))
ADD_G = False
CELL_G = False
GW = 256
ADD0, ADD1, SIG0, SIG1, CELL0, CELL1, TANH0, TANH1 = 3, 3, 4, 4, 5, 5, 6, 6


def tile_scncore_pa_kernel(
    tc, core_input, h_state, c_state, concept, W_in, W_st, W_ci, W_cs, out_0, out_1
):
    nc = tc.nc
    weights = (W_ci, W_in, W_cs, W_st)
    operands = (concept, core_input, concept, h_state)
    operand_names = ("concept", "core_input", "concept", "h_state")
    chunks = [
        (half, gate, m)
        for half in range(HALVES)
        for gate in GATE_ORDER
        for m in (FIRST_ORDER if half == 0 and gate == GATE_ORDER[0] else ORDER)
    ]
    n_chunks = len(chunks)
    h_view = out_0.rearrange("(p b) h -> p b h", b=B_TILES)
    c_view = out_1.rearrange("(p b) h -> p b h", b=B_TILES)

    with ExitStack() as ctx:
        const = ctx.enter_context(tc.tile_pool(name="const", bufs=1))
        act_pool = ctx.enter_context(tc.tile_pool(name="activations", bufs=1))
        w_pool = ctx.enter_context(tc.tile_pool(name="w_raw", bufs=PREFETCH))
        sorted_pool = ctx.enter_context(tc.tile_pool(name="sorted", bufs=AHEAD + 2))
        grouped_pool = ctx.enter_context(tc.tile_pool(name="grouped", bufs=3))
        code_pool = ctx.enter_context(tc.tile_pool(name="codes", bufs=4))
        gate_pool = ctx.enter_context(tc.tile_pool(name="gate", bufs=2))
        hidden_pool = ctx.enter_context(tc.tile_pool(name="hidden", bufs=3))
        cell_pool = ctx.enter_context(tc.tile_pool(name="cell", bufs=1))
        turn_pool = ctx.enter_context(tc.psum_pool(name="turned", bufs=TURN_BANKS))
        acc_pool = ctx.enter_context(tc.psum_pool(name="acc", bufs=8 - TURN_BANKS))

        identity = const.tile([P, P], F32, name="identity")
        masks.make_identity(nc, identity[:])

        x_raw = {}
        x_mx = {}
        w_raw = {}
        w_sorted = {}
        w_grouped = {}
        w_mx = {}
        acc_of = {}
        modulator = {}
        product = {}
        pre = {}
        hidden = {}
        cell = {}

        def load_operand(m):
            if operand_names[m] in x_raw:
                return
            raw = act_pool.tile([P, B_TILES * K], BF16, name=operand_names[m] + "_raw")
            view = operands[m].rearrange("(p b) k -> p (b k)", b=B_TILES)
            pieces = B_TILES if m == 0 else 1
            n = B_TILES * K // pieces
            for i in range(pieces):
                nc.sync.dma_start(out=raw[:, i * n : (i + 1) * n], in_=view[:, i * n : (i + 1) * n])
            x_raw[operand_names[m]] = raw

        def load_chunk(j):
            if j >= n_chunks:
                return
            half, gate, m = chunks[j]
            row0 = gate * HIDDEN + half * CHUNK
            raw = w_pool.tile([P, ROWS * K], BF16, name="w_raw")
            view = weights[m][row0 : row0 + CHUNK, :].rearrange("(c r) k -> c (r k)", r=ROWS)
            pieces = FIRST_PIECES if j < PIECED else 1
            n = ROWS * K // pieces
            for i in range(pieces):
                nc.sync.dma_start(out=raw[:, i * n : (i + 1) * n], in_=view[:, i * n : (i + 1) * n])
            w_raw[j] = raw

        def turn_operand(m):
            name = operand_names[m]
            if name in x_mx:
                return
            words = x_raw[name][:].bitcast(F32)
            grouped = act_pool.tile(
                [P, PASSES * BATCH * PACK], BF16, name=name + "_grouped", align_bytes=64
            )
            grouped_words = grouped[:].bitcast(F32).rearrange("p (s n) -> p s n", s=PASSES)
            for s in range(PASSES):
                bank = turn_pool.tile([P, BANK], F32, name="bank")
                for b in range(B_TILES):
                    for u in range(2):
                        col = b * WORDS + 2 * s * P
                        slot = (2 * b + u) * P
                        nc.tensor.transpose(
                            bank[:, slot : slot + P],
                            words[:, col + u : col + 2 * P : 2],
                            identity[:],
                        )
                (nc.vector.tensor_copy if XV else nc.scalar.copy)(
                    out=grouped_words[:, s, :].rearrange("p (b c u) -> p b c u", b=B_TILES, u=2),
                    in_=bank[:].rearrange("p (b u c) -> p b c u", b=B_TILES, u=2),
                )
            codes = act_pool.tile([P, PASSES * BATCH], U32, name=name + "_codes", align_bytes=64)
            scales = act_pool.tile([P, PASSES * BATCH], U8, name=name + "_scales", align_bytes=64)
            x_mx[name] = (codes, scales, grouped)

        def quantise_operand(m):
            name = operand_names[m]
            codes, scales, grouped = x_mx[name]
            nc.vector.quantize_mx(out=codes[:].bitcast(FP8X4), scales=scales[:], in_=grouped[:])

        def sort_chunk(j):
            if not SORT_FROM <= j < n_chunks - UNSORTED_TAIL or SORTED == 0:
                return
            w_sorted[j] = sorted_pool.tile([P, SORTED * K], BF16, name="w_sorted")
            nc.vector.tensor_copy(
                out=w_sorted[j][:].bitcast(F32).rearrange("p (g u q) -> p g u q", u=2, q=P),
                in_=w_raw[j][:, : SORTED * K]
                .bitcast(F32)
                .rearrange("p (g q u) -> p g u q", u=2, q=P),
            )

        def turn_bank(j, s, rh):
            if j >= n_chunks:
                return
            words = w_raw[j][:].bitcast(F32)
            if s == 0 and rh == 0:
                w_grouped[j] = grouped_pool.tile(
                    [P, PASSES * CHUNK * PACK], BF16, name="w_grouped", align_bytes=64
                )
            grouped_words = w_grouped[j][:].bitcast(F32).rearrange(
                "p (s c rh q) -> p s c rh q", s=PASSES, c=P, rh=2
            )
            bank = turn_pool.tile([P, BANK], F32, name="bank")
            for rl in range(2):
                for u in range(2):
                    r = 2 * rh + rl
                    col = r * WORDS + 2 * s * P
                    slot = (2 * rl + u) * P
                    if r < SORTED and SORT_FROM <= j < n_chunks - UNSORTED_TAIL:
                        block = w_sorted[j][:].bitcast(F32)[:, col + u * P : col + (u + 1) * P]
                    else:
                        block = words[:, col + u : col + 2 * P : 2]
                    nc.tensor.transpose(bank[:, slot : slot + P], block, identity[:])
            vec = LASTV and j == n_chunks - 1 and s == 1
            (nc.vector.tensor_copy if vec else nc.scalar.copy)(
                out=grouped_words[:, s, :, rh, :],
                in_=bank[:].rearrange("p (q c) -> p c q", c=P),
            )

        def quantise_pass(j, s):
            if not 0 <= j < n_chunks:
                return
            if s == 0:
                codes = code_pool.tile([P, PASSES * CHUNK], U32, name="w_codes", align_bytes=64)
                scales = code_pool.tile([P, PASSES * CHUNK], U8, name="w_scales", align_bytes=64)
                w_mx[j] = (codes, scales)
            codes, scales = w_mx[j]
            cols = slice(s * CHUNK, (s + 1) * CHUNK)
            nc.vector.quantize_mx(
                out=codes[:, cols].bitcast(FP8X4),
                scales=scales[:, cols],
                in_=w_grouped[j][:, s * CHUNK * PACK : (s + 1) * CHUNK * PACK],
            )

        def multiply_tile(j, b):
            if not 0 <= j < n_chunks:
                return
            x_codes, x_scales, x_grouped = x_mx[operand_names[chunks[j][2]]]
            w_codes, w_scales = w_mx[j]
            acc = acc_pool.tile([P, CHUNK], F32, name="acc")
            acc_of[j, b] = acc
            for s in range(PASSES):
                x_cols = slice((s * B_TILES + b) * P, (s * B_TILES + b + 1) * P)
                w_cols = slice(s * CHUNK, (s + 1) * CHUNK)
                nc.tensor.matmul_mx(
                    out=acc[:],
                    lhsT=x_codes[:, x_cols].bitcast(FP8X4),
                    lhsT_scale=x_scales[:, x_cols],
                    rhs=w_codes[:, w_cols].bitcast(FP8X4),
                    rhs_scale=w_scales[:, w_cols],
                    start=(s == 0),
                    stop=(s == PASSES - 1),
                )

        def drain_tile(j, b):
            if not 0 <= j < n_chunks:
                return
            m = chunks[j][2]
            acc = acc_of[j, b]
            if m % 2 == 0:
                if b == 0:
                    modulator[half_gate(j) + (m,)] = gate_pool.tile([P, B_TILES, CHUNK], F32, name="modulator", bufs=3)
                copy = nc.scalar.copy if (m, b) in GI_SCALAR or j >= n_chunks - LAST_S else nc.vector.tensor_copy
                copy(out=modulator[half_gate(j) + (m,)][:, b, :], in_=acc[:])
            else:
                if b == 0:
                    product[half_gate(j) + (m,)] = gate_pool.tile([P, B_TILES, CHUNK], F32, name="product%d" % m)
                nc.vector.tensor_tensor(
                    out=product[half_gate(j) + (m,)][:, b, :],
                    in0=acc[:],
                    in1=modulator[half_gate(j) + (m - 1,)][:, b, :],
                    op=ALU.mult,
                )

        def half_gate(j):
            return chunks[j][:2]

        def closes_gate(j):
            return 0 <= j < n_chunks and chunks[j][2] == len(weights) - 1

        def worker(j):
            return nc.gpsimd if ADD_G and j < n_chunks - 1 else nc.vector

        def cworker(j):
            return nc.gpsimd if CELL_G and j < n_chunks - 1 else nc.vector

        def add_products(j, b):
            if not closes_gate(j):
                return
            if b == 0:
                pre[j] = gate_pool.tile([P, B_TILES, CHUNK], F32, name="pre")
            for c0 in range(0, CHUNK, GW if worker(j) is nc.gpsimd else CHUNK):
                c1 = c0 + (GW if worker(j) is nc.gpsimd else CHUNK)
                worker(j).tensor_tensor(
                    out=pre[j][:, b, c0:c1],
                    in0=product[half_gate(j) + (1,)][:, b, c0:c1],
                    in1=product[half_gate(j) + (3,)][:, b, c0:c1],
                    op=ALU.add,
                )

        def squash_gate(j, b):
            if not closes_gate(j):
                return
            half, gate = chunks[j][0], chunks[j][1]
            if b == 0:
                hidden[half, gate] = hidden_pool.tile([P, B_TILES, CHUNK], F32, name="hidden")
            nc.scalar.activation(
                out=hidden[half, gate][:, b, :], in_=pre[j][:, b, :], func=ACT.Sigmoid
            )

        def two(j, out, in0, in1, op):
            w = cworker(j)
            n = GW if w is nc.gpsimd else CHUNK
            for c0 in range(0, CHUNK, n):
                w.tensor_tensor(out=out[:, c0:c0+n], in0=in0[:, c0:c0+n], in1=in1[:, c0:c0+n], op=op)

        def update_cell(j, b):
            if not closes_gate(j):
                return
            half, gate = chunks[j][0], chunks[j][1]
            cols = slice(half * CHUNK, (half + 1) * CHUNK)
            if gate == GATE_F:
                if b == 0:
                    cell[half, "kept"] = cell_pool.tile([P, B_TILES, CHUNK], F32, name="kept")
                two(j, cell[half, "kept"][:, b, :], hidden[half, GATE_F][:, b, :], c_prev[:, b, cols], ALU.mult)
            if gate == GATE_C:
                if b == 0:
                    cell[half, "fresh"] = cell_pool.tile([P, B_TILES, CHUNK], F32, name="fresh")
                    cell[half, "c_new"] = cell_pool.tile([P, B_TILES, CHUNK], F32, name="c_new")
                two(j, cell[half, "fresh"][:, b, :], hidden[half, GATE_I][:, b, :], hidden[half, GATE_C][:, b, :], ALU.mult)
            if gate == GATE_O:
                if b == 0:
                    cell[half, "h_new"] = cell_pool.tile([P, B_TILES, CHUNK], F32, name="h_new")
                two(j, cell[half, "h_new"][:, b, :], hidden[half, GATE_O][:, b, :], cell[half, "tanh_c"][:, b, :], ALU.mult)
                nc.sync.dma_start(out=h_view[:, b, cols], in_=cell[half, "h_new"][:, b, :])

        def update_cell2(j, b):
            if not closes_gate(j) or chunks[j][1] != GATE_C:
                return
            half = chunks[j][0]
            cols = slice(half * CHUNK, (half + 1) * CHUNK)
            two(j, cell[half, "c_new"][:, b, :], cell[half, "fresh"][:, b, :], cell[half, "kept"][:, b, :], ALU.add)
            nc.sync.dma_start(out=c_view[:, b, cols], in_=cell[half, "c_new"][:, b, :])

        def squash_cell(j, b):
            if not closes_gate(j) or chunks[j][1] != GATE_C:
                return
            half = chunks[j][0]
            if b == 0:
                cell[half, "tanh_c"] = cell_pool.tile([P, B_TILES, CHUNK], F32, name="tanh_c")
            nc.scalar.activation(
                out=cell[half, "tanh_c"][:, b, :], in_=cell[half, "c_new"][:, b, :], func=ACT.Tanh
            )

        ctx.enter_context(tc.manual_schedule())
        c_prev = act_pool.tile([P, B_TILES, HIDDEN], BF16, name="c_prev")
        for j in range(PREFETCH):
            if j == CPREV_AT:
                nc.sync.dma_start(out=c_prev[:], in_=c_state.rearrange("(p b) h -> p b h", b=B_TILES))
            if j < 4:
                load_operand(chunks[j][2])
            load_chunk(j)
        for j in range(AHEAD):
            if j == 0:
                sort_chunk(j)
        for step in range(n_chunks + 9):
            n = step
            if step < len(weights) and operand_names[chunks[step][2]] not in x_mx:
                turn_operand(chunks[step][2])
                if not XQLATE:
                    quantise_operand(chunks[step][2])
            if 0 < step < AHEAD:
                sort_chunk(step)
            turn_bank(n, 0, 0)
            turn_bank(n, 0, 1)
            quantise_pass(n - 1, 0)
            multiply_tile(n - MUL, 0)
            drain_tile(n - MUL, 0)
            add_products(n - ADD0, 0)
            add_products(n - ADD1, 1)
            squash_gate(n - SIG0, 0)
            turn_bank(n, 1, 0)
            turn_bank(n, 1, 1)
            squash_gate(n - SIG1, 1)
            squash_cell(n - TANH0, 0)
            squash_cell(n - TANH1, 1)
            load_chunk(n + PREFETCH)
            quantise_pass(n - 1, 1)
            sort_chunk(n + AHEAD)
            multiply_tile(n - MUL, 1)
            drain_tile(n - MUL, 1)
            if XQLATE and step in (0, 1, 3):
                quantise_operand(step)
            update_cell(n - CELL0, 0)
            update_cell(n - CELL1, 1)
            update_cell2(n - CELL0, 0)
            update_cell2(n - CELL1, 1)
